import numpy as np
import ml_dtypes


def mxq(x, axis, fmt="e4m3"):
    dtype, down = {"e4m3": (ml_dtypes.float8_e4m3fn, 7), "e5m2": (ml_dtypes.float8_e5m2, 14)}[fmt]
    v = np.moveaxis(np.asarray(x, np.float32).astype(ml_dtypes.bfloat16).astype(np.float64), axis, -1)
    blocks = v.reshape(v.shape[:-1] + (-1, 32))
    amax = np.abs(blocks).max(-1, keepdims=True)
    byte = np.maximum(np.where(amax > 0, np.frexp(amax)[1] - 1 + 127, 0) - down, 1)
    scale = np.exp2(byte - 127.0)
    codes = (blocks / scale).astype(np.float32).astype(dtype).astype(np.float64)
    return np.moveaxis((codes * scale).reshape(v.shape), -1, axis)


WIDE = False


def mx_kscale(k):
    if not WIDE:
        return np.ones(k)
    levels = np.array([10, -10, 5, -5, 0])
    a = np.random.permutation(np.resize(levels, k // 512 * 4)).reshape(k // 512, 4)
    idx = np.arange(k)
    return np.exp2(a[idx // 512, idx % 128 // 32])


BF16 = ml_dtypes.bfloat16


def bf(x):
    return np.asarray(x, np.float32).astype(BF16)


def f64(x):
    return np.asarray(x).astype(np.float64)


S, D, H, HD = 256, 2048, 16, 128
W = H * HD


def rotary(xq, xk, freqs):
    ll = freqs[:, :, 0:1]
    rr = freqs[:, :, 1:2]
    fl = np.concatenate([ll, ll], axis=-1).reshape(S, 1, HD)
    fr = np.concatenate([-rr, rr], axis=-1).reshape(S, 1, HD)
    xq_ = xq.reshape(S, H, HD // 2, 2).reshape(S, H, HD)
    xk_ = xk.reshape(S, H, HD // 2, 2).reshape(S, H, HD)
    return xq * fl + xq_ * fr, xk * fl + xk_ * fr


def setup_inputs():
    s = mx_kscale(D)
    c = 1.0 / np.sqrt(D)
    theta = 10000.0 ** (-np.arange(0, HD, 2) / HD)
    angles = np.arange(S)[:, None] * theta[None, :]
    return {"x": bf(np.random.standard_normal((S, D)) * s),
            "freqs": bf(np.stack([np.cos(angles), np.sin(angles)], axis=-1)),
            "wq": bf(np.random.standard_normal((W, D)) * c / s[None, :]),
            "wk": bf(np.random.standard_normal((W, D)) * c / s[None, :]),
            "wv": bf(np.random.standard_normal((W, D)) * c / s[None, :])}


def reference(x, freqs, wq, wk, wv):
    xm = mxq(f64(x), 1, "e4m3")
    xq = xm @ mxq(f64(wq), 1, "e4m3").T
    xk = xm @ mxq(f64(wk), 1, "e4m3").T
    xv = xm @ mxq(f64(wv), 1, "e4m3").T
    xq = xq.reshape(S, H, HD)
    xk = xk.reshape(S, H, HD)
    xv = xv.reshape(S, H, HD)
    xq, xk = rotary(xq, xk, f64(freqs))
    q = np.transpose(xq, (1, 0, 2))
    k = np.transpose(xk, (1, 0, 2))
    v = np.transpose(xv, (1, 0, 2))
    return q, k, v

@@ -1,0 +1,158 @@
+from contextlib import ExitStack
+
+import concourse.mybir as mybir
+from concourse.masks import make_identity
+
+BF16 = mybir.dt.bfloat16
+F32 = mybir.dt.float32
+U32 = mybir.dt.uint32
+U8 = mybir.dt.uint8
+FP8X4 = mybir.dt.float8_e4m3fn_x4
+
+P = 128
+PACK = 4
+TOKENS = 256
+FEATURES_IN = 2048
+HEADS = 16
+HEAD_DIM = 128
+PASSES = FEATURES_IN // (P * PACK)
+ROWS = 2
+GROUP = ROWS * P
+GROUP_HEADS = GROUP // HEAD_DIM
+GROUPS_PER_PROJECTION = HEADS * HEAD_DIM // GROUP
+PAIRS_PER_ROW = FEATURES_IN // 2
+HALVES = 2
+GROUP_VALUES = PASSES * GROUP * PACK
+GROUP_WORDS = PASSES * GROUP
+
+LAG = 2
+
+FLOPS = 2 * TOKENS * FEATURES_IN * 3 * HEADS * HEAD_DIM
+
+
+def tile_attention_pa_kernel(tc, x, freqs, wq, wk, wv, q_out, k_out, v_out):
+    nc = tc.nc
+    projections = ((wq, q_out, True), (wk, k_out, True), (wv, v_out, False))
+    groups = len(projections) * GROUPS_PER_PROJECTION
+
+    with ExitStack() as ctx:
+        keep = ctx.enter_context(tc.tile_pool(name="keep", bufs=1))
+        raw_pool = ctx.enter_context(tc.tile_pool(name="raw", bufs=8))
+        grouped_pool = ctx.enter_context(tc.tile_pool(name="grouped", bufs=3))
+        mx_pool = ctx.enter_context(tc.tile_pool(name="mx", bufs=LAG + 2))
+        result_pool = ctx.enter_context(tc.tile_pool(name="result", bufs=4))
+        flipped_pool = ctx.enter_context(tc.psum_pool(name="flipped", bufs=6))
+        acc_pool = ctx.enter_context(tc.psum_pool(name="acc", bufs=2))
+        ctx.enter_context(tc.manual_schedule())
+
+        identity = keep.tile([P, P], F32)
+        make_identity(nc, identity[:])
+
+        def transpose_pass(pairs, c):
+            bank = flipped_pool.tile([P, ROWS, HALVES, P], F32)
+            for r in range(ROWS):
+                for u in range(HALVES):
+                    first = r * PAIRS_PER_ROW + (HALVES * c + u) * P
+                    nc.tensor.transpose(bank[:, r, u, :], pairs[:, first : first + P], identity[:])
+            return bank
+
+        x_raw = keep.tile([P, ROWS * FEATURES_IN], BF16)
+        nc.sync.dma_start(out=x_raw[:], in_=x.rearrange("(p e) k -> p (e k)", e=ROWS))
+        angles = keep.tile([P, ROWS, HEAD_DIM // 2, 2], BF16)
+        nc.scalar.dma_start(out=angles[:], in_=freqs.rearrange("(p e) j i -> p e j i", e=ROWS))
+
+        x_grouped = keep.tile([P, GROUP_VALUES], BF16, align_bytes=64)
+        x_grouped_pairs = x_grouped[:].bitcast(F32).rearrange(
+            "k (c e p u) -> k c e p u", c=PASSES, e=ROWS, p=P, u=HALVES
+        )
+        for c in range(PASSES):
+            bank = transpose_pass(x_raw[:].bitcast(F32), c)
+            nc.vector.tensor_copy(
+                out=x_grouped_pairs[:, c, :, :, :], in_=bank[:].rearrange("k e u p -> k e p u")
+            )
+        x_codes = keep.tile([P, GROUP_WORDS], U32, align_bytes=64)
+        x_scales = keep.tile([P, GROUP_WORDS], U8, align_bytes=64)
+        nc.vector.quantize_mx(out=x_codes[:].bitcast(FP8X4), scales=x_scales[:], in_=x_grouped[:])
+
+        factor = keep.tile([P, ROWS, HEAD_DIM // 2, 2], F32)
+        cos = angles[:, :, :, 0]
+        sin = angles[:, :, :, 1]
+        nc.vector.tensor_tensor(out=factor[:, :, :, 0], in0=cos, in1=sin, op=mybir.AluOpType.subtract)
+        nc.vector.tensor_tensor(out=factor[:, :, :, 1], in0=cos, in1=sin, op=mybir.AluOpType.add)
+        factor_by_head = (
+            factor[:]
+            .rearrange("p e j i -> p e (j i)")
+            .unsqueeze(1)
+            .to_broadcast([P, GROUP_HEADS, ROWS, HEAD_DIM])
+        )
+
+        def load_and_transpose(g):
+            weight = projections[g // GROUPS_PER_PROJECTION][0]
+            first = (g % GROUPS_PER_PROJECTION) * GROUP
+            raw = raw_pool.tile([P, ROWS * FEATURES_IN], BF16)
+            nc.sync.dma_start(
+                out=raw[:],
+                in_=weight[first : first + GROUP, :].rearrange("(p r) k -> p (r k)", r=ROWS),
+            )
+            grouped = grouped_pool.tile([P, GROUP_VALUES], BF16, align_bytes=64)
+            grouped_pairs = grouped[:].bitcast(F32).rearrange(
+                "k (c p r u) -> k c p r u", c=PASSES, p=P, r=ROWS, u=HALVES
+            )
+            for c in range(PASSES):
+                bank = transpose_pass(raw[:].bitcast(F32), c)
+                nc.scalar.copy(
+                    out=grouped_pairs[:, c, :, :, :], in_=bank[:].rearrange("k r u p -> k p r u")
+                )
+            return grouped
+
+        def quantise(grouped):
+            codes = mx_pool.tile([P, GROUP_WORDS], U32, align_bytes=64)
+            scales = mx_pool.tile([P, GROUP_WORDS], U8, align_bytes=64)
+            nc.vector.quantize_mx(out=codes[:].bitcast(FP8X4), scales=scales[:], in_=grouped[:])
+            return codes, scales
+
+        def multiply(codes, scales):
+            acc = acc_pool.tile([P, ROWS, GROUP], F32)
+            for e in range(ROWS):
+                for c in range(PASSES):
+                    x_cols = slice((c * ROWS + e) * P, (c * ROWS + e + 1) * P)
+                    w_cols = slice(c * GROUP, (c + 1) * GROUP)
+                    nc.tensor.matmul_mx(
+                        out=acc[:, e, :],
+                        lhsT=x_codes[:, x_cols].bitcast(FP8X4),
+                        lhsT_scale=x_scales[:, x_cols],
+                        rhs=codes[:, w_cols].bitcast(FP8X4),
+                        rhs_scale=scales[:, w_cols],
+                        start=(c == 0),
+                        stop=(c == PASSES - 1),
+                    )
+            return acc
+
+        def finish(g, acc):
+            out, rotary = projections[g // GROUPS_PER_PROJECTION][1:]
+            first_head = (g % GROUPS_PER_PROJECTION) * GROUP_HEADS
+            result = result_pool.tile([P, GROUP_HEADS, ROWS, HEAD_DIM], F32)
+            by_head = acc[:].rearrange("p e (h d) -> p h e d", h=GROUP_HEADS)
+            if rotary:
+                nc.vector.tensor_tensor(
+                    out=result[:], in0=by_head, in1=factor_by_head, op=mybir.AluOpType.mult
+                )
+            else:
+                nc.vector.tensor_copy(out=result[:], in_=by_head)
+            nc.gpsimd.dma_start(
+                out=out[first_head : first_head + GROUP_HEADS, :, :].rearrange(
+                    "h (p e) d -> p h (e d)", e=ROWS
+                ),
+                in_=result[:].rearrange("p h e d -> p h (e d)"),
+            )
+
+        grouped_of = {}
+        operand_of = {}
+        for g in range(groups + LAG):
+            if g < groups:
+                grouped_of[g] = load_and_transpose(g)
+            if 1 <= g <= groups:
+                operand_of[g - 1] = quantise(grouped_of[g - 1])
+            if g >= LAG:
+                codes, scales = operand_of[g - LAG]
+                finish(g - LAG, multiply(codes, scales))

@@ -17,15 +17,16 @@ HEADS = 16
 HEAD_DIM = 128
 PASSES = FEATURES_IN // (P * PACK)
 ROWS = 2
-GROUP = ROWS * P
-GROUP_HEADS = GROUP // HEAD_DIM
-GROUPS_PER_PROJECTION = HEADS * HEAD_DIM // GROUP
 PAIRS_PER_ROW = FEATURES_IN // 2
 HALVES = 2
-GROUP_VALUES = PASSES * GROUP * PACK
-GROUP_WORDS = PASSES * GROUP
+SLAB = ROWS * P
+SLABS = 2
+GROUP = SLABS * SLAB
+GROUP_HEADS = GROUP // HEAD_DIM
+GROUPS_PER_PROJECTION = HEADS * HEAD_DIM // GROUP
+PASS_VALUES = GROUP * PACK
 
-LAG = 2
+AHEAD = 6
 
 FLOPS = 2 * TOKENS * FEATURES_IN * 3 * HEADS * HEAD_DIM
 
@@ -37,12 +38,12 @@ def tile_attention_pa_kernel(tc, x, freqs, wq, wk, wv, q_out, k_out, v_out):
 
     with ExitStack() as ctx:
         keep = ctx.enter_context(tc.tile_pool(name="keep", bufs=1))
-        raw_pool = ctx.enter_context(tc.tile_pool(name="raw", bufs=8))
-        grouped_pool = ctx.enter_context(tc.tile_pool(name="grouped", bufs=3))
-        mx_pool = ctx.enter_context(tc.tile_pool(name="mx", bufs=LAG + 2))
-        result_pool = ctx.enter_context(tc.tile_pool(name="result", bufs=4))
+        raw_pool = ctx.enter_context(tc.tile_pool(name="raw", bufs=SLABS + AHEAD))
+        grouped_pool = ctx.enter_context(tc.tile_pool(name="grouped", bufs=2))
+        mx_pool = ctx.enter_context(tc.tile_pool(name="mx", bufs=2))
+        result_pool = ctx.enter_context(tc.tile_pool(name="result", bufs=6))
         flipped_pool = ctx.enter_context(tc.psum_pool(name="flipped", bufs=6))
-        acc_pool = ctx.enter_context(tc.psum_pool(name="acc", bufs=2))
+        acc_pool = ctx.enter_context(tc.psum_pool(name="acc", bufs=ROWS))
         ctx.enter_context(tc.manual_schedule())
 
         identity = keep.tile([P, P], F32)
@@ -56,12 +57,25 @@ def tile_attention_pa_kernel(tc, x, freqs, wq, wk, wv, q_out, k_out, v_out):
                     nc.tensor.transpose(bank[:, r, u, :], pairs[:, first : first + P], identity[:])
             return bank
 
+        def load_slab(i):
+            weight = projections[i // (SLABS * GROUPS_PER_PROJECTION)][0]
+            first = (i % (SLABS * GROUPS_PER_PROJECTION)) * SLAB
+            raw = raw_pool.tile([P, ROWS * FEATURES_IN], BF16)
+            nc.sync.dma_start(
+                out=raw[:],
+                in_=weight[first : first + SLAB, :].rearrange("(p r) k -> p (r k)", r=ROWS),
+            )
+            return raw
+
         x_raw = keep.tile([P, ROWS * FEATURES_IN], BF16)
         nc.sync.dma_start(out=x_raw[:], in_=x.rearrange("(p e) k -> p (e k)", e=ROWS))
         angles = keep.tile([P, ROWS, HEAD_DIM // 2, 2], BF16)
         nc.scalar.dma_start(out=angles[:], in_=freqs.rearrange("(p e) j i -> p e j i", e=ROWS))
+        raw_of = {}
+        for i in range(AHEAD):
+            raw_of[i] = load_slab(i)
 
-        x_grouped = keep.tile([P, GROUP_VALUES], BF16, align_bytes=64)
+        x_grouped = keep.tile([P, PASSES * TOKENS * PACK], BF16, align_bytes=64)
         x_grouped_pairs = x_grouped[:].bitcast(F32).rearrange(
             "k (c e p u) -> k c e p u", c=PASSES, e=ROWS, p=P, u=HALVES
         )
@@ -70,8 +84,8 @@ def tile_attention_pa_kernel(tc, x, freqs, wq, wk, wv, q_out, k_out, v_out):
             nc.vector.tensor_copy(
                 out=x_grouped_pairs[:, c, :, :, :], in_=bank[:].rearrange("k e u p -> k e p u")
             )
-        x_codes = keep.tile([P, GROUP_WORDS], U32, align_bytes=64)
-        x_scales = keep.tile([P, GROUP_WORDS], U8, align_bytes=64)
+        x_codes = keep.tile([P, PASSES * TOKENS], U32, align_bytes=64)
+        x_scales = keep.tile([P, PASSES * TOKENS], U8, align_bytes=64)
         nc.vector.quantize_mx(out=x_codes[:].bitcast(FP8X4), scales=x_scales[:], in_=x_grouped[:])
 
         factor = keep.tile([P, ROWS, HEAD_DIM // 2, 2], F32)
@@ -79,46 +93,44 @@ def tile_attention_pa_kernel(tc, x, freqs, wq, wk, wv, q_out, k_out, v_out):
         sin = angles[:, :, :, 1]
         nc.vector.tensor_tensor(out=factor[:, :, :, 0], in0=cos, in1=sin, op=mybir.AluOpType.subtract)
         nc.vector.tensor_tensor(out=factor[:, :, :, 1], in0=cos, in1=sin, op=mybir.AluOpType.add)
-        factor_by_head = (
-            factor[:]
-            .rearrange("p e j i -> p e (j i)")
-            .unsqueeze(1)
-            .to_broadcast([P, GROUP_HEADS, ROWS, HEAD_DIM])
-        )
+        factor_of_token = factor[:].rearrange("p e j i -> p e (j i)")
 
-        def load_and_transpose(g):
-            weight = projections[g // GROUPS_PER_PROJECTION][0]
-            first = (g % GROUPS_PER_PROJECTION) * GROUP
-            raw = raw_pool.tile([P, ROWS * FEATURES_IN], BF16)
-            nc.sync.dma_start(
-                out=raw[:],
-                in_=weight[first : first + GROUP, :].rearrange("(p r) k -> p (r k)", r=ROWS),
-            )
-            grouped = grouped_pool.tile([P, GROUP_VALUES], BF16, align_bytes=64)
+        def transpose_and_quantise(g):
+            grouped = grouped_pool.tile([P, PASSES * PASS_VALUES], BF16, align_bytes=64)
             grouped_pairs = grouped[:].bitcast(F32).rearrange(
-                "k (c p r u) -> k c p r u", c=PASSES, p=P, r=ROWS, u=HALVES
+                "k (c a p r u) -> k c a p r u", c=PASSES, a=SLABS, p=P, r=ROWS, u=HALVES
             )
+            for a in range(SLABS):
+                pairs = raw_of[g * SLABS + a][:].bitcast(F32)
+                for c in range(PASSES):
+                    bank = transpose_pass(pairs, c)
+                    nc.scalar.copy(
+                        out=grouped_pairs[:, c, a, :, :, :],
+                        in_=bank[:].rearrange("k r u p -> k p r u"),
+                    )
+            codes = mx_pool.tile([P, PASSES * GROUP], U32, align_bytes=64)
+            scales = mx_pool.tile([P, PASSES * GROUP], U8, align_bytes=64)
             for c in range(PASSES):
-                bank = transpose_pass(raw[:].bitcast(F32), c)
-                nc.scalar.copy(
-                    out=grouped_pairs[:, c, :, :, :], in_=bank[:].rearrange("k r u p -> k p r u")
+                nc.vector.quantize_mx(
+                    out=codes[:, c * GROUP : (c + 1) * GROUP].bitcast(FP8X4),
+                    scales=scales[:, c * GROUP : (c + 1) * GROUP],
+                    in_=grouped[:, c * PASS_VALUES : (c + 1) * PASS_VALUES],
                 )
-            return grouped
-
-        def quantise(grouped):
-            codes = mx_pool.tile([P, GROUP_WORDS], U32, align_bytes=64)
-            scales = mx_pool.tile([P, GROUP_WORDS], U8, align_bytes=64)
-            nc.vector.quantize_mx(out=codes[:].bitcast(FP8X4), scales=scales[:], in_=grouped[:])
             return codes, scales
 
-        def multiply(codes, scales):
-            acc = acc_pool.tile([P, ROWS, GROUP], F32)
+        def multiply_and_store(g, codes, scales):
+            out, rotary = projections[g // GROUPS_PER_PROJECTION][1:]
+            first_head = (g % GROUPS_PER_PROJECTION) * GROUP_HEADS
+            acc_of = []
             for e in range(ROWS):
-                for c in range(PASSES):
+                acc = acc_pool.tile([P, GROUP], F32)
+                acc_of.append(acc)
+            for c in range(PASSES):
+                for e in range(ROWS):
                     x_cols = slice((c * ROWS + e) * P, (c * ROWS + e + 1) * P)
                     w_cols = slice(c * GROUP, (c + 1) * GROUP)
                     nc.tensor.matmul_mx(
-                        out=acc[:, e, :],
+                        out=acc_of[e][:],
                         lhsT=x_codes[:, x_cols].bitcast(FP8X4),
                         lhsT_scale=x_scales[:, x_cols],
                         rhs=codes[:, w_cols].bitcast(FP8X4),
@@ -126,33 +138,32 @@ def tile_attention_pa_kernel(tc, x, freqs, wq, wk, wv, q_out, k_out, v_out):
                         start=(c == 0),
                         stop=(c == PASSES - 1),
                     )
-            return acc
-
-        def finish(g, acc):
-            out, rotary = projections[g // GROUPS_PER_PROJECTION][1:]
-            first_head = (g % GROUPS_PER_PROJECTION) * GROUP_HEADS
             result = result_pool.tile([P, GROUP_HEADS, ROWS, HEAD_DIM], F32)
-            by_head = acc[:].rearrange("p e (h d) -> p h e d", h=GROUP_HEADS)
-            if rotary:
-                nc.vector.tensor_tensor(
-                    out=result[:], in0=by_head, in1=factor_by_head, op=mybir.AluOpType.mult
-                )
-            else:
-                nc.vector.tensor_copy(out=result[:], in_=by_head)
-            nc.gpsimd.dma_start(
+            for e in range(ROWS):
+                by_head = acc_of[e][:].rearrange("p (h d) -> p h d", h=GROUP_HEADS)
+                if rotary:
+                    nc.vector.tensor_tensor(
+                        out=result[:, :, e, :],
+                        in0=by_head,
+                        in1=factor_of_token[:, e, :].unsqueeze(1).to_broadcast([P, GROUP_HEADS, HEAD_DIM]),
+                        op=mybir.AluOpType.mult,
+                    )
+                else:
+                    nc.vector.tensor_copy(out=result[:, :, e, :], in_=by_head)
+            nc.sync.dma_start(
                 out=out[first_head : first_head + GROUP_HEADS, :, :].rearrange(
                     "h (p e) d -> p h (e d)", e=ROWS
                 ),
                 in_=result[:].rearrange("p h e d -> p h (e d)"),
             )
 
-        grouped_of = {}
         operand_of = {}
-        for g in range(groups + LAG):
+        for g in range(groups + 1):
             if g < groups:
-                grouped_of[g] = load_and_transpose(g)
-            if 1 <= g <= groups:
-                operand_of[g - 1] = quantise(grouped_of[g - 1])
-            if g >= LAG:
-                codes, scales = operand_of[g - LAG]
-                finish(g - LAG, multiply(codes, scales))
+                for i in range(g * SLABS + AHEAD, (g + 1) * SLABS + AHEAD):
+                    if i < groups * SLABS:
+                        raw_of[i] = load_slab(i)
+                operand_of[g] = transpose_and_quantise(g)
+            if g >= 1:
+                codes, scales = operand_of[g - 1]
+                multiply_and_store(g - 1, codes, scales)

@@ -41,7 +41,7 @@ def tile_attention_pa_kernel(tc, x, freqs, wq, wk, wv, q_out, k_out, v_out):
         raw_pool = ctx.enter_context(tc.tile_pool(name="raw", bufs=SLABS + AHEAD))
         grouped_pool = ctx.enter_context(tc.tile_pool(name="grouped", bufs=2))
         mx_pool = ctx.enter_context(tc.tile_pool(name="mx", bufs=2))
-        result_pool = ctx.enter_context(tc.tile_pool(name="result", bufs=6))
+        result_pool = ctx.enter_context(tc.tile_pool(name="result", bufs=groups))
         flipped_pool = ctx.enter_context(tc.psum_pool(name="flipped", bufs=6))
         acc_pool = ctx.enter_context(tc.psum_pool(name="acc", bufs=ROWS))
         ctx.enter_context(tc.manual_schedule())
@@ -118,9 +118,8 @@ def tile_attention_pa_kernel(tc, x, freqs, wq, wk, wv, q_out, k_out, v_out):
                 )
             return codes, scales
 
-        def multiply_and_store(g, codes, scales):
-            out, rotary = projections[g // GROUPS_PER_PROJECTION][1:]
-            first_head = (g % GROUPS_PER_PROJECTION) * GROUP_HEADS
+        def multiply(g, codes, scales):
+            rotary = projections[g // GROUPS_PER_PROJECTION][2]
             acc_of = []
             for e in range(ROWS):
                 acc = acc_pool.tile([P, GROUP], F32)
@@ -150,6 +149,11 @@ def tile_attention_pa_kernel(tc, x, freqs, wq, wk, wv, q_out, k_out, v_out):
                     )
                 else:
                     nc.vector.tensor_copy(out=result[:, :, e, :], in_=by_head)
+            return result
+
+        def store(g, result):
+            out = projections[g // GROUPS_PER_PROJECTION][1]
+            first_head = (g % GROUPS_PER_PROJECTION) * GROUP_HEADS
             nc.sync.dma_start(
                 out=out[first_head : first_head + GROUP_HEADS, :, :].rearrange(
                     "h (p e) d -> p h (e d)", e=ROWS
@@ -158,6 +162,7 @@ def tile_attention_pa_kernel(tc, x, freqs, wq, wk, wv, q_out, k_out, v_out):
             )
 
         operand_of = {}
+        result_of = {}
         for g in range(groups + 1):
             if g < groups:
                 for i in range(g * SLABS + AHEAD, (g + 1) * SLABS + AHEAD):
@@ -166,4 +171,6 @@ def tile_attention_pa_kernel(tc, x, freqs, wq, wk, wv, q_out, k_out, v_out):
                 operand_of[g] = transpose_and_quantise(g)
             if g >= 1:
                 codes, scales = operand_of[g - 1]
-                multiply_and_store(g - 1, codes, scales)
+                result_of[g - 1] = multiply(g - 1, codes, scales)
+        for g in range(groups):
+            store(g, result_of[g])

@@ -49,13 +49,14 @@ def tile_attention_pa_kernel(tc, x, freqs, wq, wk, wv, q_out, k_out, v_out):
         identity = keep.tile([P, P], F32)
         make_identity(nc, identity[:])
 
-        def transpose_pass(pairs, c):
+        def transpose_pass(raw, c, copy, out):
+            pairs = raw[:].bitcast(F32)
             bank = flipped_pool.tile([P, ROWS, HALVES, P], F32)
             for r in range(ROWS):
                 for u in range(HALVES):
                     first = r * PAIRS_PER_ROW + (HALVES * c + u) * P
                     nc.tensor.transpose(bank[:, r, u, :], pairs[:, first : first + P], identity[:])
-            return bank
+            copy(out=out, in_=bank[:].rearrange("k r u p -> k r p u"))
 
         def load_slab(i):
             weight = projections[i // (SLABS * GROUPS_PER_PROJECTION)][0]
@@ -80,10 +81,7 @@ def tile_attention_pa_kernel(tc, x, freqs, wq, wk, wv, q_out, k_out, v_out):
             "k (c e p u) -> k c e p u", c=PASSES, e=ROWS, p=P, u=HALVES
         )
         for c in range(PASSES):
-            bank = transpose_pass(x_raw[:].bitcast(F32), c)
-            nc.vector.tensor_copy(
-                out=x_grouped_pairs[:, c, :, :, :], in_=bank[:].rearrange("k e u p -> k e p u")
-            )
+            transpose_pass(x_raw, c, nc.vector.tensor_copy, x_grouped_pairs[:, c, :, :, :])
         x_codes = keep.tile([P, PASSES * TOKENS], U32, align_bytes=64)
         x_scales = keep.tile([P, PASSES * TOKENS], U8, align_bytes=64)
         nc.vector.quantize_mx(out=x_codes[:].bitcast(FP8X4), scales=x_scales[:], in_=x_grouped[:])
@@ -93,21 +91,17 @@ def tile_attention_pa_kernel(tc, x, freqs, wq, wk, wv, q_out, k_out, v_out):
         sin = angles[:, :, :, 1]
         nc.vector.tensor_tensor(out=factor[:, :, :, 0], in0=cos, in1=sin, op=mybir.AluOpType.subtract)
         nc.vector.tensor_tensor(out=factor[:, :, :, 1], in0=cos, in1=sin, op=mybir.AluOpType.add)
-        factor_of_token = factor[:].rearrange("p e j i -> p e (j i)")
 
         def transpose_and_quantise(g):
             grouped = grouped_pool.tile([P, PASSES * PASS_VALUES], BF16, align_bytes=64)
             grouped_pairs = grouped[:].bitcast(F32).rearrange(
-                "k (c a p r u) -> k c a p r u", c=PASSES, a=SLABS, p=P, r=ROWS, u=HALVES
+                "k (c r a p u) -> k c r a p u", c=PASSES, r=ROWS, a=SLABS, p=P, u=HALVES
             )
             for a in range(SLABS):
-                pairs = raw_of[g * SLABS + a][:].bitcast(F32)
                 for c in range(PASSES):
-                    bank = transpose_pass(pairs, c)
-                    nc.scalar.copy(
-                        out=grouped_pairs[:, c, a, :, :, :],
-                        in_=bank[:].rearrange("k r u p -> k p r u"),
-                    )
+                    first_wanted = a == SLABS - 1 and c == 0
+                    copy = nc.vector.tensor_copy if first_wanted else nc.scalar.copy
+                    transpose_pass(raw_of[g * SLABS + a], c, copy, grouped_pairs[:, c, :, a, :, :])
             codes = mx_pool.tile([P, PASSES * GROUP], U32, align_bytes=64)
             scales = mx_pool.tile([P, PASSES * GROUP], U8, align_bytes=64)
             for c in range(PASSES):
@@ -139,16 +133,19 @@ def tile_attention_pa_kernel(tc, x, freqs, wq, wk, wv, q_out, k_out, v_out):
                     )
             result = result_pool.tile([P, GROUP_HEADS, ROWS, HEAD_DIM], F32)
             for e in range(ROWS):
-                by_head = acc_of[e][:].rearrange("p (h d) -> p h d", h=GROUP_HEADS)
+                product = acc_of[e][:].rearrange("p (r h j) -> p h j r", r=ROWS, h=GROUP_HEADS)
+                in_order = result[:, :, e, :].rearrange("p h (j r) -> p h j r", r=ROWS)
                 if rotary:
                     nc.vector.tensor_tensor(
-                        out=result[:, :, e, :],
-                        in0=by_head,
-                        in1=factor_of_token[:, e, :].unsqueeze(1).to_broadcast([P, GROUP_HEADS, HEAD_DIM]),
+                        out=in_order,
+                        in0=product,
+                        in1=factor[:, e, :, :]
+                        .unsqueeze(1)
+                        .to_broadcast([P, GROUP_HEADS, HEAD_DIM // 2, ROWS]),
                         op=mybir.AluOpType.mult,
                     )
                 else:
-                    nc.vector.tensor_copy(out=result[:, :, e, :], in_=by_head)
+                    nc.vector.tensor_copy(out=in_order, in_=product)
             return result
 
         def store(g, result):

@@ -20,28 +20,33 @@ ROWS = 2
 PAIRS_PER_ROW = FEATURES_IN // 2
 HALVES = 2
 SLAB = ROWS * P
-SLABS = 2
-GROUP = SLABS * SLAB
-GROUP_HEADS = GROUP // HEAD_DIM
-GROUPS_PER_PROJECTION = HEADS * HEAD_DIM // GROUP
-PASS_VALUES = GROUP * PACK
+SLAB_HEADS = SLAB // HEAD_DIM
+SLABS_PER_PROJECTION = HEADS * HEAD_DIM // SLAB
+PROJECTIONS = 3
+SLABS = PROJECTIONS * SLABS_PER_PROJECTION
+WIDEST = 2
 
+LONE_FIRST = 4
+LONE_LAST = 0
 AHEAD = 6
 
-FLOPS = 2 * TOKENS * FEATURES_IN * 3 * HEADS * HEAD_DIM
+FLOPS = 2 * TOKENS * FEATURES_IN * PROJECTIONS * HEADS * HEAD_DIM
 
 
 def tile_attention_pa_kernel(tc, x, freqs, wq, wk, wv, q_out, k_out, v_out):
     nc = tc.nc
     projections = ((wq, q_out, True), (wk, k_out, True), (wv, v_out, False))
-    groups = len(projections) * GROUPS_PER_PROJECTION
+    groups = (
+        [(i, 1) for i in range(LONE_FIRST)]
+        + [(i, WIDEST) for i in range(LONE_FIRST, SLABS - LONE_LAST, WIDEST)]
+        + [(i, 1) for i in range(SLABS - LONE_LAST, SLABS)]
+    )
 
     with ExitStack() as ctx:
         keep = ctx.enter_context(tc.tile_pool(name="keep", bufs=1))
-        raw_pool = ctx.enter_context(tc.tile_pool(name="raw", bufs=SLABS + AHEAD))
+        raw_pool = ctx.enter_context(tc.tile_pool(name="raw", bufs=WIDEST + AHEAD))
         grouped_pool = ctx.enter_context(tc.tile_pool(name="grouped", bufs=2))
         mx_pool = ctx.enter_context(tc.tile_pool(name="mx", bufs=2))
-        result_pool = ctx.enter_context(tc.tile_pool(name="result", bufs=groups))
         flipped_pool = ctx.enter_context(tc.psum_pool(name="flipped", bufs=6))
         acc_pool = ctx.enter_context(tc.psum_pool(name="acc", bufs=ROWS))
         ctx.enter_context(tc.manual_schedule())
@@ -59,8 +64,8 @@ def tile_attention_pa_kernel(tc, x, freqs, wq, wk, wv, q_out, k_out, v_out):
             copy(out=out, in_=bank[:].rearrange("k r u p -> k r p u"))
 
         def load_slab(i):
-            weight = projections[i // (SLABS * GROUPS_PER_PROJECTION)][0]
-            first = (i % (SLABS * GROUPS_PER_PROJECTION)) * SLAB
+            weight = projections[i // SLABS_PER_PROJECTION][0]
+            first = (i % SLABS_PER_PROJECTION) * SLAB
             raw = raw_pool.tile([P, ROWS * FEATURES_IN], BF16)
             nc.sync.dma_start(
                 out=raw[:],
@@ -92,38 +97,49 @@ def tile_attention_pa_kernel(tc, x, freqs, wq, wk, wv, q_out, k_out, v_out):
         nc.vector.tensor_tensor(out=factor[:, :, :, 0], in0=cos, in1=sin, op=mybir.AluOpType.subtract)
         nc.vector.tensor_tensor(out=factor[:, :, :, 1], in0=cos, in1=sin, op=mybir.AluOpType.add)
 
-        def transpose_and_quantise(g):
-            grouped = grouped_pool.tile([P, PASSES * PASS_VALUES], BF16, align_bytes=64)
-            grouped_pairs = grouped[:].bitcast(F32).rearrange(
-                "k (c r a p u) -> k c r a p u", c=PASSES, r=ROWS, a=SLABS, p=P, u=HALVES
-            )
-            for a in range(SLABS):
-                for c in range(PASSES):
-                    first_wanted = a == SLABS - 1 and c == 0
-                    copy = nc.vector.tensor_copy if first_wanted else nc.scalar.copy
-                    transpose_pass(raw_of[g * SLABS + a], c, copy, grouped_pairs[:, c, :, a, :, :])
-            codes = mx_pool.tile([P, PASSES * GROUP], U32, align_bytes=64)
-            scales = mx_pool.tile([P, PASSES * GROUP], U8, align_bytes=64)
-            for c in range(PASSES):
-                nc.vector.quantize_mx(
-                    out=codes[:, c * GROUP : (c + 1) * GROUP].bitcast(FP8X4),
-                    scales=scales[:, c * GROUP : (c + 1) * GROUP],
-                    in_=grouped[:, c * PASS_VALUES : (c + 1) * PASS_VALUES],
-                )
-            return codes, scales
+        result_of = []
+        for j in range(PROJECTIONS):
+            result = keep.tile([P, HEADS, ROWS, HEAD_DIM], F32, name="result%d" % j)
+            result_of.append(result)
 
-        def multiply(g, codes, scales):
-            rotary = projections[g // GROUPS_PER_PROJECTION][2]
+        def transpose_group(g):
+            first, slabs = groups[g]
+            width = slabs * SLAB
+            grouped = grouped_pool.tile([P, PASSES * width * PACK], BF16, align_bytes=64)
+            grouped_pairs = grouped[:].bitcast(F32).rearrange(
+                "k (c r a p u) -> k c r a p u", c=PASSES, r=ROWS, a=slabs, p=P, u=HALVES
+            )
+            for a in range(slabs):
+                for c in range(PASSES):
+                    first_wanted = slabs > 1 and a == slabs - 1 and c == 0
+                    copy = nc.vector.tensor_copy if first_wanted else nc.scalar.copy
+                    transpose_pass(raw_of[first + a], c, copy, grouped_pairs[:, c, :, a, :, :])
+            codes = mx_pool.tile([P, PASSES * width], U32, align_bytes=64)
+            scales = mx_pool.tile([P, PASSES * width], U8, align_bytes=64)
+            return grouped, codes, scales
+
+        def quantise_pass(g, c, operand):
+            width = groups[g][1] * SLAB
+            grouped, codes, scales = operand
+            nc.vector.quantize_mx(
+                out=codes[:, c * width : (c + 1) * width].bitcast(FP8X4),
+                scales=scales[:, c * width : (c + 1) * width],
+                in_=grouped[:, c * width * PACK : (c + 1) * width * PACK],
+            )
+
+        def multiply(g, operand):
+            width = groups[g][1] * SLAB
+            grouped, codes, scales = operand
             acc_of = []
             for e in range(ROWS):
-                acc = acc_pool.tile([P, GROUP], F32)
+                acc = acc_pool.tile([P, WIDEST * SLAB], F32)
                 acc_of.append(acc)
             for c in range(PASSES):
                 for e in range(ROWS):
                     x_cols = slice((c * ROWS + e) * P, (c * ROWS + e + 1) * P)
-                    w_cols = slice(c * GROUP, (c + 1) * GROUP)
+                    w_cols = slice(c * width, (c + 1) * width)
                     nc.tensor.matmul_mx(
-                        out=acc_of[e][:],
+                        out=acc_of[e][:, 0:width],
                         lhsT=x_codes[:, x_cols].bitcast(FP8X4),
                         lhsT_scale=x_scales[:, x_cols],
                         rhs=codes[:, w_cols].bitcast(FP8X4),
@@ -131,43 +147,57 @@ def tile_attention_pa_kernel(tc, x, freqs, wq, wk, wv, q_out, k_out, v_out):
                         start=(c == 0),
                         stop=(c == PASSES - 1),
                     )
-            result = result_pool.tile([P, GROUP_HEADS, ROWS, HEAD_DIM], F32)
+            return acc_of
+
+        def take_out(g, acc_of):
+            first, slabs = groups[g]
+            width = slabs * SLAB
+            heads = slabs * SLAB_HEADS
+            j = first // SLABS_PER_PROJECTION
+            rotary = projections[j][2]
+            first_head = (first % SLABS_PER_PROJECTION) * SLAB_HEADS
             for e in range(ROWS):
-                product = acc_of[e][:].rearrange("p (r h j) -> p h j r", r=ROWS, h=GROUP_HEADS)
-                in_order = result[:, :, e, :].rearrange("p h (j r) -> p h j r", r=ROWS)
+                product = acc_of[e][:, 0:width].rearrange("p (r h j) -> p h j r", r=ROWS, h=heads)
+                in_order = result_of[j][:, first_head : first_head + heads, e, :].rearrange(
+                    "p h (j r) -> p h j r", r=ROWS
+                )
                 if rotary:
                     nc.vector.tensor_tensor(
                         out=in_order,
                         in0=product,
-                        in1=factor[:, e, :, :]
-                        .unsqueeze(1)
-                        .to_broadcast([P, GROUP_HEADS, HEAD_DIM // 2, ROWS]),
+                        in1=factor[:, e, :, :].unsqueeze(1).to_broadcast([P, heads, HEAD_DIM // 2, ROWS]),
                         op=mybir.AluOpType.mult,
                     )
                 else:
                     nc.vector.tensor_copy(out=in_order, in_=product)
-            return result
 
-        def store(g, result):
-            out = projections[g // GROUPS_PER_PROJECTION][1]
-            first_head = (g % GROUPS_PER_PROJECTION) * GROUP_HEADS
+        def store(g):
+            first, slabs = groups[g]
+            heads = slabs * SLAB_HEADS
+            j = first // SLABS_PER_PROJECTION
+            first_head = (first % SLABS_PER_PROJECTION) * SLAB_HEADS
             nc.sync.dma_start(
-                out=out[first_head : first_head + GROUP_HEADS, :, :].rearrange(
+                out=projections[j][1][first_head : first_head + heads, :, :].rearrange(
                     "h (p e) d -> p h (e d)", e=ROWS
                 ),
-                in_=result[:].rearrange("p h e d -> p h (e d)"),
+                in_=result_of[j][:, first_head : first_head + heads, :, :].rearrange("p h e d -> p h (e d)"),
             )
 
         operand_of = {}
-        result_of = {}
-        for g in range(groups + 1):
-            if g < groups:
-                for i in range(g * SLABS + AHEAD, (g + 1) * SLABS + AHEAD):
-                    if i < groups * SLABS:
+        for g in range(len(groups) + 1):
+            lone = g < len(groups) and groups[g][1] == 1
+            if g < len(groups):
+                first, slabs = groups[g]
+                for i in range(first + AHEAD, first + slabs + AHEAD):
+                    if i < SLABS:
                         raw_of[i] = load_slab(i)
-                operand_of[g] = transpose_and_quantise(g)
+                operand_of[g] = transpose_group(g)
+                for c in range(PASSES - 1 if lone else PASSES):
+                    quantise_pass(g, c, operand_of[g])
             if g >= 1:
-                codes, scales = operand_of[g - 1]
-                result_of[g - 1] = multiply(g - 1, codes, scales)
-        for g in range(groups):
-            store(g, result_of[g])
+                acc_of = multiply(g - 1, operand_of[g - 1])
+                take_out(g - 1, acc_of)
+            if lone:
+                quantise_pass(g, PASSES - 1, operand_of[g])
+        for g in range(len(groups)):
+            store(g)

@@ -27,8 +27,9 @@ SLABS = PROJECTIONS * SLABS_PER_PROJECTION
 WIDEST = 2
 
 LONE_FIRST = 4
-LONE_LAST = 0
+LONE_LAST = 2
 AHEAD = 6
+WARM_UP = 8
 
 FLOPS = 2 * TOKENS * FEATURES_IN * PROJECTIONS * HEADS * HEAD_DIM
 
@@ -53,6 +54,12 @@ def tile_attention_pa_kernel(tc, x, freqs, wq, wk, wv, q_out, k_out, v_out):
 
         identity = keep.tile([P, P], F32)
         make_identity(nc, identity[:])
+
+        zeros = keep.tile([P, WIDEST * SLAB], BF16)
+        nc.vector.memset(zeros[:], 0.0)
+        idle = acc_pool.tile([P, WIDEST * SLAB], F32, name="acc")
+        for i in range(WARM_UP):
+            nc.tensor.matmul(idle[:], lhsT=zeros[:, 0:P], rhs=zeros[:], start=True, stop=True)
 
         def transpose_pass(raw, c, copy, out):
             pairs = raw[:].bitcast(F32)
@@ -168,6 +175,8 @@ def tile_attention_pa_kernel(tc, x, freqs, wq, wk, wv, q_out, k_out, v_out):
                         in1=factor[:, e, :, :].unsqueeze(1).to_broadcast([P, heads, HEAD_DIM // 2, ROWS]),
                         op=mybir.AluOpType.mult,
                     )
+                elif e == 0:
+                    nc.scalar.copy(out=in_order, in_=product)
                 else:
                     nc.vector.tensor_copy(out=in_order, in_=product)
 

@@ -26,7 +26,7 @@ PROJECTIONS = 3
 SLABS = PROJECTIONS * SLABS_PER_PROJECTION
 WIDEST = 2
 
-LONE_FIRST = 4
+ROUND_SLABS = (1, 1, 1, 1, 2, 2, 2, 2, 2, 2, 2, 2, 2, 2)
 LONE_LAST = 2
 AHEAD = 6
 WARM_UP = 8
@@ -37,19 +37,23 @@ FLOPS = 2 * TOKENS * FEATURES_IN * PROJECTIONS * HEADS * HEAD_DIM
 def tile_attention_pa_kernel(tc, x, freqs, wq, wk, wv, q_out, k_out, v_out):
     nc = tc.nc
     projections = ((wq, q_out, True), (wk, k_out, True), (wv, v_out, False))
-    groups = (
-        [(i, 1) for i in range(LONE_FIRST)]
-        + [(i, WIDEST) for i in range(LONE_FIRST, SLABS - LONE_LAST, WIDEST)]
-        + [(i, 1) for i in range(SLABS - LONE_LAST, SLABS)]
-    )
+    rounds = []
+    for size in ROUND_SLABS:
+        start = sum(ROUND_SLABS[0 : len(rounds)])
+        found = []
+        for i in range(start, start + size):
+            if size == 1 or i >= SLABS - LONE_LAST:
+                found.append((i, 1))
+            elif i % WIDEST == 0:
+                found.append((i, WIDEST))
+        rounds.append(found)
 
     with ExitStack() as ctx:
         keep = ctx.enter_context(tc.tile_pool(name="keep", bufs=1))
-        raw_pool = ctx.enter_context(tc.tile_pool(name="raw", bufs=WIDEST + AHEAD))
+        raw_pool = ctx.enter_context(tc.tile_pool(name="raw", bufs=max(ROUND_SLABS) + AHEAD))
         grouped_pool = ctx.enter_context(tc.tile_pool(name="grouped", bufs=2))
-        mx_pool = ctx.enter_context(tc.tile_pool(name="mx", bufs=2))
-        flipped_pool = ctx.enter_context(tc.psum_pool(name="flipped", bufs=6))
-        acc_pool = ctx.enter_context(tc.psum_pool(name="acc", bufs=ROWS))
+        mx_pool = ctx.enter_context(tc.tile_pool(name="mx", bufs=4))
+        psum = ctx.enter_context(tc.psum_pool(name="psum", bufs=8))
         ctx.enter_context(tc.manual_schedule())
 
         identity = keep.tile([P, P], F32)
@@ -57,13 +61,13 @@ def tile_attention_pa_kernel(tc, x, freqs, wq, wk, wv, q_out, k_out, v_out):
 
         zeros = keep.tile([P, WIDEST * SLAB], BF16)
         nc.vector.memset(zeros[:], 0.0)
-        idle = acc_pool.tile([P, WIDEST * SLAB], F32, name="acc")
+        idle = psum.tile([P, WIDEST * SLAB], F32, name="bank")
         for i in range(WARM_UP):
             nc.tensor.matmul(idle[:], lhsT=zeros[:, 0:P], rhs=zeros[:], start=True, stop=True)
 
         def transpose_pass(raw, c, copy, out):
             pairs = raw[:].bitcast(F32)
-            bank = flipped_pool.tile([P, ROWS, HALVES, P], F32)
+            bank = psum.tile([P, ROWS, HALVES, P], F32, name="bank")
             for r in range(ROWS):
                 for u in range(HALVES):
                     first = r * PAIRS_PER_ROW + (HALVES * c + u) * P
@@ -109,8 +113,8 @@ def tile_attention_pa_kernel(tc, x, freqs, wq, wk, wv, q_out, k_out, v_out):
             result = keep.tile([P, HEADS, ROWS, HEAD_DIM], F32, name="result%d" % j)
             result_of.append(result)
 
-        def transpose_group(g):
-            first, slabs = groups[g]
+        def transpose_group(group):
+            first, slabs = group
             width = slabs * SLAB
             grouped = grouped_pool.tile([P, PASSES * width * PACK], BF16, align_bytes=64)
             grouped_pairs = grouped[:].bitcast(F32).rearrange(
@@ -125,8 +129,8 @@ def tile_attention_pa_kernel(tc, x, freqs, wq, wk, wv, q_out, k_out, v_out):
             scales = mx_pool.tile([P, PASSES * width], U8, align_bytes=64)
             return grouped, codes, scales
 
-        def quantise_pass(g, c, operand):
-            width = groups[g][1] * SLAB
+        def quantise_pass(group, c, operand):
+            width = group[1] * SLAB
             grouped, codes, scales = operand
             nc.vector.quantize_mx(
                 out=codes[:, c * width : (c + 1) * width].bitcast(FP8X4),
@@ -134,12 +138,12 @@ def tile_attention_pa_kernel(tc, x, freqs, wq, wk, wv, q_out, k_out, v_out):
                 in_=grouped[:, c * width * PACK : (c + 1) * width * PACK],
             )
 
-        def multiply(g, operand):
-            width = groups[g][1] * SLAB
+        def multiply(group, operand):
+            width = group[1] * SLAB
             grouped, codes, scales = operand
             acc_of = []
             for e in range(ROWS):
-                acc = acc_pool.tile([P, WIDEST * SLAB], F32)
+                acc = psum.tile([P, WIDEST * SLAB], F32, name="bank")
                 acc_of.append(acc)
             for c in range(PASSES):
                 for e in range(ROWS):
@@ -156,8 +160,8 @@ def tile_attention_pa_kernel(tc, x, freqs, wq, wk, wv, q_out, k_out, v_out):
                     )
             return acc_of
 
-        def take_out(g, acc_of):
-            first, slabs = groups[g]
+        def take_out(group, acc_of):
+            first, slabs = group
             width = slabs * SLAB
             heads = slabs * SLAB_HEADS
             j = first // SLABS_PER_PROJECTION
@@ -180,8 +184,8 @@ def tile_attention_pa_kernel(tc, x, freqs, wq, wk, wv, q_out, k_out, v_out):
                 else:
                     nc.vector.tensor_copy(out=in_order, in_=product)
 
-        def store(g):
-            first, slabs = groups[g]
+        def store(group):
+            first, slabs = group
             heads = slabs * SLAB_HEADS
             j = first // SLABS_PER_PROJECTION
             first_head = (first % SLABS_PER_PROJECTION) * SLAB_HEADS
@@ -193,20 +197,25 @@ def tile_attention_pa_kernel(tc, x, freqs, wq, wk, wv, q_out, k_out, v_out):
             )
 
         operand_of = {}
-        for g in range(len(groups) + 1):
-            lone = g < len(groups) and groups[g][1] == 1
-            if g < len(groups):
-                first, slabs = groups[g]
+        for t in range(len(rounds) + 1):
+            now = rounds[t] if t < len(rounds) else []
+            before = rounds[t - 1] if t >= 1 else []
+            lone = len(now) == 1 and now[0][1] == 1
+            for group in now:
+                first, slabs = group
                 for i in range(first + AHEAD, first + slabs + AHEAD):
                     if i < SLABS:
                         raw_of[i] = load_slab(i)
-                operand_of[g] = transpose_group(g)
+                operand_of[group] = transpose_group(group)
                 for c in range(PASSES - 1 if lone else PASSES):
-                    quantise_pass(g, c, operand_of[g])
-            if g >= 1:
-                acc_of = multiply(g - 1, operand_of[g - 1])
-                take_out(g - 1, acc_of)
+                    quantise_pass(group, c, operand_of[group])
+            acc_of = {}
+            for group in before:
+                acc_of[group] = multiply(group, operand_of[group])
+            for group in before:
+                take_out(group, acc_of[group])
             if lone:
-                quantise_pass(g, PASSES - 1, operand_of[g])
-        for g in range(len(groups)):
-            store(g)
+                quantise_pass(now[0], PASSES - 1, operand_of[now[0]])
+        for found in rounds:
+            for group in found:
+                store(group)

@@ -200,22 +200,21 @@ def tile_attention_pa_kernel(tc, x, freqs, wq, wk, wv, q_out, k_out, v_out):
         for t in range(len(rounds) + 1):
             now = rounds[t] if t < len(rounds) else []
             before = rounds[t - 1] if t >= 1 else []
-            lone = len(now) == 1 and now[0][1] == 1
             for group in now:
                 first, slabs = group
                 for i in range(first + AHEAD, first + slabs + AHEAD):
                     if i < SLABS:
                         raw_of[i] = load_slab(i)
                 operand_of[group] = transpose_group(group)
-                for c in range(PASSES - 1 if lone else PASSES):
+                for c in range(PASSES - 1 if group == now[-1] else PASSES):
                     quantise_pass(group, c, operand_of[group])
             acc_of = {}
             for group in before:
                 acc_of[group] = multiply(group, operand_of[group])
             for group in before:
                 take_out(group, acc_of[group])
-            if lone:
-                quantise_pass(now[0], PASSES - 1, operand_of[now[0]])
+            if now:
+                quantise_pass(now[-1], PASSES - 1, operand_of[now[-1]])
         for found in rounds:
             for group in found:
                 store(group)

@@ -53,7 +53,8 @@ def tile_attention_pa_kernel(tc, x, freqs, wq, wk, wv, q_out, k_out, v_out):
         raw_pool = ctx.enter_context(tc.tile_pool(name="raw", bufs=max(ROUND_SLABS) + AHEAD))
         grouped_pool = ctx.enter_context(tc.tile_pool(name="grouped", bufs=2))
         mx_pool = ctx.enter_context(tc.tile_pool(name="mx", bufs=4))
-        psum = ctx.enter_context(tc.psum_pool(name="psum", bufs=8))
+        flipped_pool = ctx.enter_context(tc.psum_pool(name="flipped", bufs=6))
+        acc_pool = ctx.enter_context(tc.psum_pool(name="acc", bufs=ROWS))
         ctx.enter_context(tc.manual_schedule())
 
         identity = keep.tile([P, P], F32)
@@ -61,13 +62,13 @@ def tile_attention_pa_kernel(tc, x, freqs, wq, wk, wv, q_out, k_out, v_out):
 
         zeros = keep.tile([P, WIDEST * SLAB], BF16)
         nc.vector.memset(zeros[:], 0.0)
-        idle = psum.tile([P, WIDEST * SLAB], F32, name="bank")
+        idle = acc_pool.tile([P, WIDEST * SLAB], F32, name="acc")
         for i in range(WARM_UP):
             nc.tensor.matmul(idle[:], lhsT=zeros[:, 0:P], rhs=zeros[:], start=True, stop=True)
 
         def transpose_pass(raw, c, copy, out):
             pairs = raw[:].bitcast(F32)
-            bank = psum.tile([P, ROWS, HALVES, P], F32, name="bank")
+            bank = flipped_pool.tile([P, ROWS, HALVES, P], F32, name="bank")
             for r in range(ROWS):
                 for u in range(HALVES):
                     first = r * PAIRS_PER_ROW + (HALVES * c + u) * P
@@ -138,12 +139,15 @@ def tile_attention_pa_kernel(tc, x, freqs, wq, wk, wv, q_out, k_out, v_out):
                 in_=grouped[:, c * width * PACK : (c + 1) * width * PACK],
             )
 
-        def multiply(group, operand):
+        def multiply(group, operand, last_round):
             width = group[1] * SLAB
             grouped, codes, scales = operand
             acc_of = []
             for e in range(ROWS):
-                acc = psum.tile([P, WIDEST * SLAB], F32, name="bank")
+                if last_round:
+                    acc = flipped_pool.tile([P, WIDEST * SLAB], F32, name="bank")
+                else:
+                    acc = acc_pool.tile([P, WIDEST * SLAB], F32, name="acc")
                 acc_of.append(acc)
             for c in range(PASSES):
                 for e in range(ROWS):
@@ -210,7 +214,7 @@ def tile_attention_pa_kernel(tc, x, freqs, wq, wk, wv, q_out, k_out, v_out):
                     quantise_pass(group, c, operand_of[group])
             acc_of = {}
             for group in before:
-                acc_of[group] = multiply(group, operand_of[group])
+                acc_of[group] = multiply(group, operand_of[group], t == len(rounds))
             for group in before:
                 take_out(group, acc_of[group])
             if now:

@@ -29,7 +29,6 @@ WIDEST = 2
 ROUND_SLABS = (1, 1, 1, 1, 2, 2, 2, 2, 2, 2, 2, 2, 2, 2)
 LONE_LAST = 2
 AHEAD = 6
-WARM_UP = 8
 
 FLOPS = 2 * TOKENS * FEATURES_IN * PROJECTIONS * HEADS * HEAD_DIM
 
@@ -59,12 +58,6 @@ def tile_attention_pa_kernel(tc, x, freqs, wq, wk, wv, q_out, k_out, v_out):
 
         identity = keep.tile([P, P], F32)
         make_identity(nc, identity[:])
-
-        zeros = keep.tile([P, WIDEST * SLAB], BF16)
-        nc.vector.memset(zeros[:], 0.0)
-        idle = acc_pool.tile([P, WIDEST * SLAB], F32, name="acc")
-        for i in range(WARM_UP):
-            nc.tensor.matmul(idle[:], lhsT=zeros[:, 0:P], rhs=zeros[:], start=True, stop=True)
 
         def transpose_pass(raw, c, copy, out):
             pairs = raw[:].bitcast(F32)

from contextlib import ExitStack

import concourse.mybir as mybir
from concourse.masks import make_identity

BF16 = mybir.dt.bfloat16
F32 = mybir.dt.float32
U32 = mybir.dt.uint32
U8 = mybir.dt.uint8
FP8X4 = mybir.dt.float8_e4m3fn_x4

P = 128
PACK = 4
TOKENS = 256
FEATURES_IN = 2048
HEADS = 16
HEAD_DIM = 128
PASSES = FEATURES_IN // (P * PACK)
ROWS = 2
PAIRS_PER_ROW = FEATURES_IN // 2
HALVES = 2
SLAB = ROWS * P
SLAB_HEADS = SLAB // HEAD_DIM
SLABS_PER_PROJECTION = HEADS * HEAD_DIM // SLAB
PROJECTIONS = 3
SLABS = PROJECTIONS * SLABS_PER_PROJECTION
WIDEST = 2

ROUND_SLABS = (1, 1, 1, 1, 2, 2, 2, 2, 2, 2, 2, 2, 2, 2)
LONE_LAST = 2
AHEAD = 6

FLOPS = 2 * TOKENS * FEATURES_IN * PROJECTIONS * HEADS * HEAD_DIM


def tile_attention_pa_kernel(tc, x, freqs, wq, wk, wv, q_out, k_out, v_out):
    nc = tc.nc
    projections = ((wq, q_out, True), (wk, k_out, True), (wv, v_out, False))
    rounds = []
    for size in ROUND_SLABS:
        start = sum(ROUND_SLABS[0 : len(rounds)])
        found = []
        for i in range(start, start + size):
            if size == 1 or i >= SLABS - LONE_LAST:
                found.append((i, 1))
            elif i % WIDEST == 0:
                found.append((i, WIDEST))
        rounds.append(found)

    with ExitStack() as ctx:
        keep = ctx.enter_context(tc.tile_pool(name="keep", bufs=1))
        raw_pool = ctx.enter_context(tc.tile_pool(name="raw", bufs=max(ROUND_SLABS) + AHEAD))
        grouped_pool = ctx.enter_context(tc.tile_pool(name="grouped", bufs=2))
        mx_pool = ctx.enter_context(tc.tile_pool(name="mx", bufs=4))
        flipped_pool = ctx.enter_context(tc.psum_pool(name="flipped", bufs=6))
        acc_pool = ctx.enter_context(tc.psum_pool(name="acc", bufs=ROWS))
        ctx.enter_context(tc.manual_schedule())

        identity = keep.tile([P, P], F32)
        make_identity(nc, identity[:])

        def transpose_pass(raw, c, copy, out):
            pairs = raw[:].bitcast(F32)
            bank = flipped_pool.tile([P, ROWS, HALVES, P], F32, name="bank")
            for r in range(ROWS):
                for u in range(HALVES):
                    first = r * PAIRS_PER_ROW + (HALVES * c + u) * P
                    nc.tensor.transpose(bank[:, r, u, :], pairs[:, first : first + P], identity[:])
            copy(out=out, in_=bank[:].rearrange("k r u p -> k r p u"))

        def load_slab(i):
            weight = projections[i // SLABS_PER_PROJECTION][0]
            first = (i % SLABS_PER_PROJECTION) * SLAB
            raw = raw_pool.tile([P, ROWS * FEATURES_IN], BF16)
            nc.sync.dma_start(
                out=raw[:],
                in_=weight[first : first + SLAB, :].rearrange("(p r) k -> p (r k)", r=ROWS),
            )
            return raw

        x_raw = keep.tile([P, ROWS * FEATURES_IN], BF16)
        nc.sync.dma_start(out=x_raw[:], in_=x.rearrange("(p e) k -> p (e k)", e=ROWS))
        angles = keep.tile([P, ROWS, HEAD_DIM // 2, 2], BF16)
        nc.scalar.dma_start(out=angles[:], in_=freqs.rearrange("(p e) j i -> p e j i", e=ROWS))
        raw_of = {}
        for i in range(AHEAD):
            raw_of[i] = load_slab(i)

        x_grouped = keep.tile([P, PASSES * TOKENS * PACK], BF16, align_bytes=64)
        x_grouped_pairs = x_grouped[:].bitcast(F32).rearrange(
            "k (c e p u) -> k c e p u", c=PASSES, e=ROWS, p=P, u=HALVES
        )
        for c in range(PASSES):
            transpose_pass(x_raw, c, nc.vector.tensor_copy, x_grouped_pairs[:, c, :, :, :])
        x_codes = keep.tile([P, PASSES * TOKENS], U32, align_bytes=64)
        x_scales = keep.tile([P, PASSES * TOKENS], U8, align_bytes=64)
        nc.vector.quantize_mx(out=x_codes[:].bitcast(FP8X4), scales=x_scales[:], in_=x_grouped[:])

        factor = keep.tile([P, ROWS, HEAD_DIM // 2, 2], F32)
        cos = angles[:, :, :, 0]
        sin = angles[:, :, :, 1]
        nc.vector.tensor_tensor(out=factor[:, :, :, 0], in0=cos, in1=sin, op=mybir.AluOpType.subtract)
        nc.vector.tensor_tensor(out=factor[:, :, :, 1], in0=cos, in1=sin, op=mybir.AluOpType.add)

        result_of = []
        for j in range(PROJECTIONS):
            result = keep.tile([P, HEADS, ROWS, HEAD_DIM], F32, name="result%d" % j)
            result_of.append(result)

        def transpose_group(group):
            first, slabs = group
            width = slabs * SLAB
            grouped = grouped_pool.tile([P, PASSES * width * PACK], BF16, align_bytes=64)
            grouped_pairs = grouped[:].bitcast(F32).rearrange(
                "k (c r a p u) -> k c r a p u", c=PASSES, r=ROWS, a=slabs, p=P, u=HALVES
            )
            for a in range(slabs):
                for c in range(PASSES):
                    first_wanted = slabs > 1 and a == slabs - 1 and c == 0
                    copy = nc.vector.tensor_copy if first_wanted else nc.scalar.copy
                    transpose_pass(raw_of[first + a], c, copy, grouped_pairs[:, c, :, a, :, :])
            codes = mx_pool.tile([P, PASSES * width], U32, align_bytes=64)
            scales = mx_pool.tile([P, PASSES * width], U8, align_bytes=64)
            return grouped, codes, scales

        def quantise_pass(group, c, operand):
            width = group[1] * SLAB
            grouped, codes, scales = operand
            nc.vector.quantize_mx(
                out=codes[:, c * width : (c + 1) * width].bitcast(FP8X4),
                scales=scales[:, c * width : (c + 1) * width],
                in_=grouped[:, c * width * PACK : (c + 1) * width * PACK],
            )

        def multiply(group, operand, last_round):
            width = group[1] * SLAB
            grouped, codes, scales = operand
            acc_of = []
            for e in range(ROWS):
                if last_round:
                    acc = flipped_pool.tile([P, WIDEST * SLAB], F32, name="bank")
                else:
                    acc = acc_pool.tile([P, WIDEST * SLAB], F32, name="acc")
                acc_of.append(acc)
            for c in range(PASSES):
                for e in range(ROWS):
                    x_cols = slice((c * ROWS + e) * P, (c * ROWS + e + 1) * P)
                    w_cols = slice(c * width, (c + 1) * width)
                    nc.tensor.matmul_mx(
                        out=acc_of[e][:, 0:width],
                        lhsT=x_codes[:, x_cols].bitcast(FP8X4),
                        lhsT_scale=x_scales[:, x_cols],
                        rhs=codes[:, w_cols].bitcast(FP8X4),
                        rhs_scale=scales[:, w_cols],
                        start=(c == 0),
                        stop=(c == PASSES - 1),
                    )
            return acc_of

        def take_out(group, acc_of):
            first, slabs = group
            width = slabs * SLAB
            heads = slabs * SLAB_HEADS
            j = first // SLABS_PER_PROJECTION
            rotary = projections[j][2]
            first_head = (first % SLABS_PER_PROJECTION) * SLAB_HEADS
            for e in range(ROWS):
                product = acc_of[e][:, 0:width].rearrange("p (r h j) -> p h j r", r=ROWS, h=heads)
                in_order = result_of[j][:, first_head : first_head + heads, e, :].rearrange(
                    "p h (j r) -> p h j r", r=ROWS
                )
                if rotary:
                    nc.vector.tensor_tensor(
                        out=in_order,
                        in0=product,
                        in1=factor[:, e, :, :].unsqueeze(1).to_broadcast([P, heads, HEAD_DIM // 2, ROWS]),
                        op=mybir.AluOpType.mult,
                    )
                elif e == 0:
                    nc.scalar.copy(out=in_order, in_=product)
                else:
                    nc.vector.tensor_copy(out=in_order, in_=product)

        def store(group):
            first, slabs = group
            heads = slabs * SLAB_HEADS
            j = first // SLABS_PER_PROJECTION
            first_head = (first % SLABS_PER_PROJECTION) * SLAB_HEADS
            nc.sync.dma_start(
                out=projections[j][1][first_head : first_head + heads, :, :].rearrange(
                    "h (p e) d -> p h (e d)", e=ROWS
                ),
                in_=result_of[j][:, first_head : first_head + heads, :, :].rearrange("p h e d -> p h (e d)"),
            )

        operand_of = {}
        for t in range(len(rounds) + 1):
            now = rounds[t] if t < len(rounds) else []
            before = rounds[t - 1] if t >= 1 else []
            for group in now:
                first, slabs = group
                for i in range(first + AHEAD, first + slabs + AHEAD):
                    if i < SLABS:
                        raw_of[i] = load_slab(i)
                operand_of[group] = transpose_group(group)
                for c in range(PASSES - 1 if group == now[-1] else PASSES):
                    quantise_pass(group, c, operand_of[group])
            acc_of = {}
            for group in before:
                acc_of[group] = multiply(group, operand_of[group], t == len(rounds))
            for group in before:
                take_out(group, acc_of[group])
            if now:
                quantise_pass(now[-1], PASSES - 1, operand_of[now[-1]])
        for found in rounds:
            for group in found:
                store(group)
